import numpy as np
import ml_dtypes


def mxq(x, axis, fmt="e4m3"):
    dtype, down = {"e4m3": (ml_dtypes.float8_e4m3fn, 7), "e5m2": (ml_dtypes.float8_e5m2, 14)}[fmt]
    v = np.moveaxis(np.asarray(x, np.float32).astype(ml_dtypes.bfloat16).astype(np.float64), axis, -1)
    blocks = v.reshape(v.shape[:-1] + (-1, 32))
    amax = np.abs(blocks).max(-1, keepdims=True)
    byte = np.maximum(np.where(amax > 0, np.frexp(amax)[1] - 1 + 127, 0) - down, 1)
    scale = np.exp2(byte - 127.0)
    codes = (blocks / scale).astype(np.float32).astype(dtype).astype(np.float64)
    return np.moveaxis((codes * scale).reshape(v.shape), -1, axis)


WIDE = False


def mx_kscale(k):
    if not WIDE:
        return np.ones(k)
    levels = np.array([10, -10, 5, -5, 0])
    if k % 512:
        return np.exp2(np.random.permutation(np.resize(levels, k // 32))).repeat(32)
    a = np.empty((k // 512, 16))
    for p in range(k // 512):
        a[p, :8] = np.random.permutation(np.resize(levels, 8))
        for g in range(8):
            far = levels[np.abs(levels - a[p, g]) >= 10]
            a[p, g + 8] = far[np.random.randint(len(far))]
    return np.exp2(a.ravel()).repeat(32)


BF16 = ml_dtypes.bfloat16


def bf(x):
    return np.asarray(x, np.float32).astype(BF16)


def f64(x):
    return np.asarray(x).astype(np.float64)


L, T, F, D = 4, 128, 1536, 512


def setup_inputs():
    s, t = mx_kscale(D), mx_kscale(F)
    return {"x": bf(np.random.standard_normal((L, T, D)) * s),
            "W_enc": bf(np.random.standard_normal((L, F, D)) / np.sqrt(D) / s * t[:, None]),
            "b_enc": bf(np.random.standard_normal((L, F)) * 0.2 * t),
            "b_dec": bf(np.random.standard_normal((L, D)) * 0.3),
            "W_dec": bf(np.random.standard_normal((L, L, F, D)) / np.sqrt(F) / t[:, None]),
            "dec_mask": np.triu(np.ones((L, L), dtype=bool))}


def reference(x, W_enc, b_enc, b_dec, W_dec, dec_mask):
    pre = f64(bf(mxq(f64(x), 2, "e4m3") @ mxq(f64(W_enc), 2, "e4m3").transpose(0, 2, 1)))
    acts = np.maximum(pre + f64(b_enc)[:, None, :], 0.0)
    aq = mxq(acts, 2, "e4m3")
    Wd = f64(W_dec)
    keep = np.asarray(dec_mask)
    recon = []
    for j in range(L):
        src = np.nonzero(keep[:, j])[0]
        a = np.concatenate([aq[i] for i in src], axis=1)
        w = mxq(Wd[src, j], 1, "e4m3").reshape(len(src) * F, D)
        recon.append((a @ w) + f64(b_dec)[j])
    return np.stack(recon)

@@ -1,0 +1,335 @@
+from contextlib import ExitStack
+
+import concourse.mybir as mybir
+from concourse.masks import make_identity
+
+F32 = mybir.dt.float32
+BF16 = mybir.dt.bfloat16
+U32 = mybir.dt.uint32
+U8 = mybir.dt.uint8
+FP8X4 = mybir.dt.float8_e4m3fn_x4
+ADD = mybir.AluOpType.add
+
+L, T, F, D = 4, 128, 1536, 512
+P = 128
+PACK = 4
+K_PASS = P * PACK
+G = F // K_PASS
+HALF = D // 2
+ENC_BANK = BF16
+
+N_BLOCKS = L * (L + 1) // 2
+FLOPS = 2 * L * T * F * D + 2 * N_BLOCKS * T * F * D
+BYTES = 2 * (L * T * D + L * F * D + L * F + L * D + N_BLOCKS * F * D) + 4 * L * T * D
+
+LOOKAHEAD = 4
+BDEC_ROUND = 7
+FIRST_OUTPUT_ROUND = BDEC_ROUND + 1
+MAX_PAIRS_A_ROUND = 2
+RUN = 4
+SCALAR_COLUMNS = (
+    [(192, 0), (448, 0), (512, 0), (512, 0), (512, 0)]
+    + [(512, 144), (512, 0), (512, 0), (512, 224), (512, 96)]
+    + [(512, 0), (512, 144), (512, 0), (512, 320), (512, 256)]
+)
+
+
+def tile_crosslayertranscoder_kernel(tc, x, W_enc, b_enc, b_dec, W_dec, dec_mask, out):
+    nc = tc.nc
+    enc_chunks = [None] + [(l, g) for l in range(L) for g in range(G)]
+    dec_chunks = [(i, j, g) for i in range(L) for j in range(i, L) for g in range(G)]
+    n_enc = len(enc_chunks)
+    n_pairs = len(dec_chunks) // 2
+    layer_finished_in = {G * l + G + 2: l for l in range(L)}
+
+    with ExitStack() as ctx:
+        keep = ctx.enter_context(tc.tile_pool(name="keep", bufs=1))
+        raw_pool = ctx.enter_context(tc.tile_pool(name="raw_pool", bufs=3 * (LOOKAHEAD + 1)))
+        enc_pool = ctx.enter_context(tc.tile_pool(name="enc_pool", bufs=2))
+        act_pool = ctx.enter_context(tc.tile_pool(name="act_pool", bufs=2))
+        out_pool = ctx.enter_context(tc.tile_pool(name="out_pool", bufs=2))
+        grouped_pool = ctx.enter_context(tc.tile_pool(name="grouped_pool", bufs=3))
+        code_pool = ctx.enter_context(tc.tile_pool(name="code_pool", bufs=5))
+        turn_pool = ctx.enter_context(tc.psum_pool(name="turn_pool", bufs=2))
+        bank_pool = ctx.enter_context(tc.psum_pool(name="bank_pool", bufs=1))
+        acc_pool = ctx.enter_context(tc.psum_pool(name="acc_pool", bufs=1))
+        ctx.enter_context(tc.manual_schedule())
+
+        benc_rows = keep.tile([P, K_PASS], BF16, name="benc_rows")
+        nc.gpsimd.memset(benc_rows[:], 0.0)
+        nc.scalar.dma_start(
+            out=benc_rows[0 : L * G, :], in_=b_enc.rearrange("l (g c) -> (l g) c", g=G)
+        )
+        ident = keep.tile([P, P], F32, name="ident")
+        make_identity(nc, ident[:])
+        benc = keep.tile([P, L * G, PACK], BF16, name="benc")
+        bdec = keep.tile([P, L * D], BF16, name="bdec")
+        x_codes = keep.tile([P, L * T], U32, name="x_codes", align_bytes=64)
+        x_scales = keep.tile([P, L * T], U8, name="x_scales", align_bytes=64)
+
+        enc_raw = {}
+        enc_turned = {}
+        enc_grouped = {}
+        enc_codes = {0: (x_codes, x_scales)}
+        enc_bank = {}
+        biased = {}
+        acts = {}
+        act_codes = {}
+        dec_raw = {}
+        dec_grouped = {}
+        dec_codes = {}
+        acc = {}
+        staged = {}
+
+        def load_enc(n):
+            if n == 0:
+                raw = keep.tile([P, L, D], BF16, name="x_raw")
+                rows = x.rearrange("l t k -> t l k")
+            else:
+                raw = raw_pool.tile([P, PACK, D], BF16, name="raw", tag="raw")
+                l, g = enc_chunks[n]
+                rows = W_enc[l, g * K_PASS : (g + 1) * K_PASS, :].rearrange(
+                    "(m s) k -> m s k", s=PACK
+                )
+            nc.sync.dma_start(out=raw[:], in_=rows)
+            enc_raw[n] = raw
+
+        def load_dec(c):
+            i, j, g = dec_chunks[c]
+            raw = raw_pool.tile([P, PACK, D], BF16, name="raw", tag="raw")
+            nc.sync.dma_start(
+                out=raw[:],
+                in_=W_dec[i, j, g * K_PASS : (g + 1) * K_PASS, :].rearrange(
+                    "(p t) d -> p t d", t=PACK
+                ),
+            )
+            dec_raw[c] = raw
+
+        def load_for_round(r):
+            if r == 0:
+                load_enc(0)
+            if r < n_pairs:
+                load_dec(2 * r)
+                load_dec(2 * r + 1)
+            if r == BDEC_ROUND:
+                nc.sync.dma_start(
+                    out=bdec[:], in_=b_dec.rearrange("l d -> (l d)").partition_broadcast(P)
+                )
+            if r + 1 < n_enc:
+                load_enc(r + 1)
+
+        def every_2nd_word(row_of_k, u):
+            return row_of_k.bitcast(F32)[:, u : D // 2 : 2]
+
+        def transpose_chunk(n):
+            banks = []
+            for h in range(2):
+                turned = turn_pool.tile([P, 2, 2, P], F32, name="turned", tag="turned")
+                for s in range(2):
+                    for u in range(2):
+                        nc.tensor.transpose(
+                            turned[:, s, u, :],
+                            every_2nd_word(enc_raw[n][:, 2 * h + s, :], u),
+                            ident[:],
+                        )
+                banks.append(turned)
+            enc_turned[n] = banks
+
+        def empty_transposes(n):
+            grouped = enc_pool.tile(
+                [P, PACK, P, PACK], BF16, name="enc_grouped", tag="enc_grouped", align_bytes=64
+            )
+            words = grouped[:].bitcast(F32)
+            for h in range(2):
+                nc.scalar.copy(
+                    out=words[:, 2 * h : 2 * h + 2, :, :],
+                    in_=enc_turned[n][h][:].rearrange("q s u m -> q s m u"),
+                )
+            enc_grouped[n] = grouped
+
+        def quantize_chunk(n):
+            if n > 0:
+                codes = enc_pool.tile([P, K_PASS], U32, name="w_codes", tag="w_codes", align_bytes=64)
+                scales = enc_pool.tile(
+                    [P, K_PASS], U8, name="w_scales", tag="w_scales", align_bytes=64
+                )
+                enc_codes[n] = (codes, scales)
+            codes, scales = enc_codes[n]
+            nc.vector.quantize_mx(
+                out=codes[:].bitcast(FP8X4),
+                scales=scales[:],
+                in_=enc_grouped[n][:].rearrange("q s m j -> q (s m j)"),
+            )
+
+        def encode_chunk(n):
+            l, g = enc_chunks[n]
+            codes, scales = enc_codes[n]
+            bank = bank_pool.tile([P, PACK, T], ENC_BANK, name="bank", tag="bank")
+            for s in range(PACK):
+                nc.tensor.matmul_mx(
+                    out=bank[:, s, :],
+                    lhsT=codes[:, s * P : (s + 1) * P].bitcast(FP8X4),
+                    lhsT_scale=scales[:, s * P : (s + 1) * P],
+                    rhs=x_codes[:, l * T : (l + 1) * T].bitcast(FP8X4),
+                    rhs_scale=x_scales[:, l * T : (l + 1) * T],
+                    start=True,
+                    stop=True,
+                )
+            enc_bank[n] = bank
+
+        def add_benc(n):
+            l, g = enc_chunks[n]
+            if g == 0:
+                biased[l] = act_pool.tile([P, G, T, PACK], BF16, name="biased", tag="biased")
+            nc.vector.tensor_tensor(
+                out=biased[l][:, g, :, :],
+                in0=enc_bank[n][:].rearrange("p s n -> p n s"),
+                in1=benc[:, n - 1 : n, :].to_broadcast([P, T, PACK]),
+                op=ADD,
+            )
+
+        def relu_layer(l):
+            acts[l] = act_pool.tile([P, G * T * PACK], BF16, name="acts", tag="acts", align_bytes=64)
+            nc.vector.tensor_scalar_max(
+                out=acts[l][:], in0=biased[l][:].rearrange("p g n s -> p (g n s)"), scalar1=0.0
+            )
+
+        def quantize_acts(l):
+            codes = keep.tile([P, G * T], U32, name="a_codes%d" % l, align_bytes=64)
+            scales = keep.tile([P, G * T], U8, name="a_scales%d" % l, align_bytes=64)
+            for lo, hi in ((0, 2 * T), (2 * T, 3 * T)):
+                nc.vector.quantize_mx(
+                    out=codes[:, lo:hi].bitcast(FP8X4),
+                    scales=scales[:, lo:hi],
+                    in_=acts[l][:, lo * PACK : hi * PACK],
+                )
+            act_codes[l] = (codes, scales)
+
+        def interleave_columns(engine_copy, grouped, h, raw, lo, hi):
+            engine_copy(
+                out=grouped[:, h, lo:hi, :].rearrange("p (c i) t -> p c t i", i=RUN),
+                in_=raw[:, :, lo:hi].rearrange("p t (c i) -> p c t i", i=RUN),
+            )
+
+        def interleave_pair(r):
+            grouped = grouped_pool.tile(
+                [P, 2, D, PACK], BF16, name="dec_grouped", tag="dec_grouped", align_bytes=64
+            )
+            dec_grouped[r] = grouped
+            for h in range(2):
+                raw = dec_raw[2 * r + h]
+                split = SCALAR_COLUMNS[r][h]
+                if split > 0:
+                    interleave_columns(nc.scalar.copy, grouped, h, raw, 0, split)
+                if split < D:
+                    interleave_columns(nc.vector.tensor_copy, grouped, h, raw, split, D)
+
+        def quantize_pair(r, pieces):
+            if r not in dec_codes:
+                codes = code_pool.tile([P, 2 * D], U32, name="d_codes", tag="d_codes", align_bytes=64)
+                scales = code_pool.tile(
+                    [P, 2 * D], U8, name="d_scales", tag="d_scales", align_bytes=64
+                )
+                dec_codes[r] = (codes, scales)
+            codes, scales = dec_codes[r]
+            grouped = dec_grouped[r][:].rearrange("p h d t -> p (h d t)")
+            for lo, hi in pieces:
+                nc.vector.quantize_mx(
+                    out=codes[:, lo:hi].bitcast(FP8X4),
+                    scales=scales[:, lo:hi],
+                    in_=grouped[:, lo * PACK : hi * PACK],
+                )
+
+        def decode_pair(r):
+            closed = []
+            codes, scales = dec_codes[r]
+            for h in range(2):
+                i, j, g = dec_chunks[2 * r + h]
+                first = i == 0 and g == 0
+                final = i == j and g == G - 1
+                parts = ((0, D),) if j < L - 1 else ((HALF, D), (0, HALF))
+                a_codes, a_scales = act_codes[i]
+                for lo, hi in parts:
+                    if first:
+                        acc[(j, lo)] = acc_pool.tile([P, hi - lo], F32, name="acc%d_%d" % (j, lo))
+                    nc.tensor.matmul_mx(
+                        out=acc[(j, lo)][:],
+                        lhsT=a_codes[:, g * T : (g + 1) * T].bitcast(FP8X4),
+                        lhsT_scale=a_scales[:, g * T : (g + 1) * T],
+                        rhs=codes[:, h * D + lo : h * D + hi].bitcast(FP8X4),
+                        rhs_scale=scales[:, h * D + lo : h * D + hi],
+                        start=first,
+                        stop=final,
+                    )
+                    if final:
+                        closed.append((j, lo, hi))
+            return closed
+
+        def add_bdec_and_store(j, lo, hi):
+            if j not in staged:
+                staged[j] = out_pool.tile([P, D], F32, name="staged", tag="staged")
+            nc.vector.tensor_tensor(
+                out=staged[j][:, lo:hi],
+                in0=acc[(j, lo)][:],
+                in1=bdec[:, j * D + lo : j * D + hi],
+                op=ADD,
+            )
+            if lo == 0:
+                nc.sync.dma_start(out=out[j], in_=staged[j][:])
+
+        benc_turned = bank_pool.tile([P, 2, P], F32, name="benc_turned", tag="bank")
+        for r in range(LOOKAHEAD):
+            load_for_round(r)
+        transpose_chunk(0)
+
+        next_pair = 0
+        outputs_due = {}
+        for r in range(n_pairs + 1):
+            load_for_round(r + LOOKAHEAD)
+            n = r - 1
+            finished = layer_finished_in.get(r)
+            if r < n_enc:
+                empty_transposes(r)
+            if 0 <= n < n_enc:
+                quantize_chunk(n)
+            if 1 <= n < n_enc:
+                encode_chunk(n)
+            if r + 1 < n_enc:
+                transpose_chunk(r + 1)
+            if r == 1:
+                for u in range(2):
+                    nc.tensor.transpose(
+                        benc_turned[:, u, :], every_2nd_word(benc_rows[:], u), ident[:]
+                    )
+            if finished is not None:
+                relu_layer(finished)
+            if r < n_pairs:
+                interleave_pair(r)
+            if 1 <= r < n_pairs:
+                quantize_pair(r - 1, ((0, 2 * D),))
+            if r == n_pairs:
+                quantize_pair(r - 1, ((0, D),))
+            if r == 1:
+                nc.vector.tensor_copy(
+                    out=benc[:].bitcast(F32),
+                    in_=benc_turned[:, :, 0 : L * G].rearrange("p u c -> p c u"),
+                )
+            if finished is not None:
+                quantize_acts(finished)
+            if r == n_pairs:
+                quantize_pair(r - 1, ((D + HALF, 2 * D), (D, D + HALF)))
+            written = 0
+            while (
+                written < MAX_PAIRS_A_ROUND
+                and next_pair < r
+                and all(dec_chunks[2 * next_pair + h][0] in act_codes for h in range(2))
+            ):
+                for group in decode_pair(next_pair):
+                    when = r if r == n_pairs else max(r + 1, FIRST_OUTPUT_ROUND)
+                    outputs_due.setdefault(when, []).append(group)
+                next_pair += 1
+                written += 1
+            if 1 <= n < n_enc:
+                add_benc(n)
+            for j, lo, hi in outputs_due.get(r, []):
+                add_bdec_and_store(j, lo, hi)

@@ -23,13 +23,14 @@ FLOPS = 2 * L * T * F * D + 2 * N_BLOCKS * T * F * D
 BYTES = 2 * (L * T * D + L * F * D + L * F + L * D + N_BLOCKS * F * D) + 4 * L * T * D
 
 LOOKAHEAD = 4
-BDEC_ROUND = 7
+BDEC_ROUND = 5
 FIRST_OUTPUT_ROUND = BDEC_ROUND + 1
 MAX_PAIRS_A_ROUND = 2
 RUN = 4
+PASSED_COLUMNS = 128
 SCALAR_COLUMNS = (
     [(192, 0), (448, 0), (512, 0), (512, 0), (512, 0)]
-    + [(512, 144), (512, 0), (512, 0), (512, 224), (512, 96)]
+    + [(512, 144), (512, 96), (512, 0), (512, 144), (512, 96)]
     + [(512, 0), (512, 144), (512, 0), (512, 320), (512, 256)]
 )
 
@@ -53,6 +54,7 @@ def tile_crosslayertranscoder_kernel(tc, x, W_enc, b_enc, b_dec, W_dec, dec_mask
         turn_pool = ctx.enter_context(tc.psum_pool(name="turn_pool", bufs=2))
         bank_pool = ctx.enter_context(tc.psum_pool(name="bank_pool", bufs=1))
         acc_pool = ctx.enter_context(tc.psum_pool(name="acc_pool", bufs=1))
+        passed_pool = ctx.enter_context(tc.psum_pool(name="passed_pool", bufs=1))
         ctx.enter_context(tc.manual_schedule())
 
         benc_rows = keep.tile([P, K_PASS], BF16, name="benc_rows")
@@ -62,6 +64,8 @@ def tile_crosslayertranscoder_kernel(tc, x, W_enc, b_enc, b_dec, W_dec, dec_mask
         )
         ident = keep.tile([P, P], F32, name="ident")
         make_identity(nc, ident[:])
+        ident_bf16 = keep.tile([P, P], BF16, name="ident_bf16")
+        make_identity(nc, ident_bf16[:])
         benc = keep.tile([P, L * G, PACK], BF16, name="benc")
         bdec = keep.tile([P, L * D], BF16, name="bdec")
         x_codes = keep.tile([P, L * T], U32, name="x_codes", align_bytes=64)
@@ -77,6 +81,7 @@ def tile_crosslayertranscoder_kernel(tc, x, W_enc, b_enc, b_dec, W_dec, dec_mask
         act_codes = {}
         dec_raw = {}
         dec_grouped = {}
+        dec_passed = {}
         dec_codes = {}
         acc = {}
         staged = {}
@@ -211,16 +216,32 @@ def tile_crosslayertranscoder_kernel(tc, x, W_enc, b_enc, b_dec, W_dec, dec_mask
                 in_=raw[:, :, lo:hi].rearrange("p t (c i) -> p c t i", i=RUN),
             )
 
-        def interleave_pair(r):
+        def pass_columns(r):
+            passed = passed_pool.tile([P, PASSED_COLUMNS, PACK], BF16, name="passed", tag="passed")
+            nc.tensor.matmul(
+                out=passed[:],
+                lhsT=ident_bf16[:],
+                rhs=dec_raw[2 * r][:, :, 0:PASSED_COLUMNS].rearrange("p t d -> p d t"),
+                start=True,
+                stop=True,
+            )
+            dec_passed[r] = passed
+
+        def start_pair(r):
             grouped = grouped_pool.tile(
                 [P, 2, D, PACK], BF16, name="dec_grouped", tag="dec_grouped", align_bytes=64
             )
             dec_grouped[r] = grouped
+            nc.scalar.copy(out=grouped[:, 0, 0:PASSED_COLUMNS, :], in_=dec_passed[r][:])
+
+        def interleave_pair(r):
+            grouped = dec_grouped[r]
             for h in range(2):
                 raw = dec_raw[2 * r + h]
                 split = SCALAR_COLUMNS[r][h]
-                if split > 0:
-                    interleave_columns(nc.scalar.copy, grouped, h, raw, 0, split)
+                done = PASSED_COLUMNS if h == 0 else 0
+                if split > done:
+                    interleave_columns(nc.scalar.copy, grouped, h, raw, done, split)
                 if split < D:
                     interleave_columns(nc.vector.tensor_copy, grouped, h, raw, split, D)
 
@@ -251,7 +272,8 @@ def tile_crosslayertranscoder_kernel(tc, x, W_enc, b_enc, b_dec, W_dec, dec_mask
                 a_codes, a_scales = act_codes[i]
                 for lo, hi in parts:
                     if first:
-                        acc[(j, lo)] = acc_pool.tile([P, hi - lo], F32, name="acc%d_%d" % (j, lo))
+                        bank_of = "acc0_0" if (j, lo) == (L - 1, 0) else "acc%d_%d" % (j, lo)
+                        acc[(j, lo)] = acc_pool.tile([P, hi - lo], F32, name="acc", tag=bank_of)
                     nc.tensor.matmul_mx(
                         out=acc[(j, lo)][:],
                         lhsT=a_codes[:, g * T : (g + 1) * T].bitcast(FP8X4),
@@ -281,6 +303,7 @@ def tile_crosslayertranscoder_kernel(tc, x, W_enc, b_enc, b_dec, W_dec, dec_mask
         for r in range(LOOKAHEAD):
             load_for_round(r)
         transpose_chunk(0)
+        pass_columns(0)
 
         next_pair = 0
         outputs_due = {}
@@ -288,12 +311,16 @@ def tile_crosslayertranscoder_kernel(tc, x, W_enc, b_enc, b_dec, W_dec, dec_mask
             load_for_round(r + LOOKAHEAD)
             n = r - 1
             finished = layer_finished_in.get(r)
+            if r < n_pairs:
+                start_pair(r)
             if r < n_enc:
                 empty_transposes(r)
             if 0 <= n < n_enc:
                 quantize_chunk(n)
             if 1 <= n < n_enc:
                 encode_chunk(n)
+            if r + 1 < n_pairs:
+                pass_columns(r + 1)
             if r + 1 < n_enc:
                 transpose_chunk(r + 1)
             if r == 1:

@@ -29,9 +29,9 @@ MAX_PAIRS_A_ROUND = 2
 RUN = 4
 PASSED_COLUMNS = 128
 SCALAR_COLUMNS = (
-    [(192, 0), (448, 0), (512, 0), (512, 0), (512, 0)]
-    + [(512, 144), (512, 96), (512, 0), (512, 144), (512, 96)]
-    + [(512, 0), (512, 144), (512, 0), (512, 320), (512, 256)]
+    [(192, 0), (448, 0), (512, 64), (512, 64), (512, 64)]
+    + [(512, 208), (512, 160), (512, 64), (512, 208), (512, 160)]
+    + [(512, 64), (512, 208), (512, 64), (512, 384), (512, 320)]
 )
 
 
@@ -311,18 +311,18 @@ def tile_crosslayertranscoder_kernel(tc, x, W_enc, b_enc, b_dec, W_dec, dec_mask
             load_for_round(r + LOOKAHEAD)
             n = r - 1
             finished = layer_finished_in.get(r)
-            if r < n_pairs:
-                start_pair(r)
             if r < n_enc:
                 empty_transposes(r)
+            if r < n_pairs:
+                start_pair(r)
             if 0 <= n < n_enc:
                 quantize_chunk(n)
             if 1 <= n < n_enc:
                 encode_chunk(n)
-            if r + 1 < n_pairs:
-                pass_columns(r + 1)
             if r + 1 < n_enc:
                 transpose_chunk(r + 1)
+            if r + 1 < n_pairs:
+                pass_columns(r + 1)
             if r == 1:
                 for u in range(2):
                     nc.tensor.transpose(

@@ -23,13 +23,14 @@ FLOPS = 2 * L * T * F * D + 2 * N_BLOCKS * T * F * D
 BYTES = 2 * (L * T * D + L * F * D + L * F + L * D + N_BLOCKS * F * D) + 4 * L * T * D
 
 LOOKAHEAD = 4
-BDEC_ROUND = 5
-FIRST_OUTPUT_ROUND = BDEC_ROUND + 1
+BDEC_ROUNDS = (2, 3)
+FIRST_OUTPUT_ROUND = 6
 MAX_PAIRS_A_ROUND = 2
 RUN = 4
 PASSED_COLUMNS = 128
+PASSED_PAIRS = 12
 SCALAR_COLUMNS = (
-    [(192, 0), (448, 0), (512, 64), (512, 64), (512, 64)]
+    [(192, 0), (448, 0), (512, 0), (512, 0), (512, 64)]
     + [(512, 208), (512, 160), (512, 64), (512, 208), (512, 160)]
     + [(512, 64), (512, 208), (512, 64), (512, 384), (512, 320)]
 )
@@ -62,6 +63,7 @@ def tile_crosslayertranscoder_kernel(tc, x, W_enc, b_enc, b_dec, W_dec, dec_mask
         nc.scalar.dma_start(
             out=benc_rows[0 : L * G, :], in_=b_enc.rearrange("l (g c) -> (l g) c", g=G)
         )
+        nc.scalar.dma_start(out=benc_rows[L * G : L * G + L, :], in_=b_dec)
         ident = keep.tile([P, P], F32, name="ident")
         make_identity(nc, ident[:])
         ident_bf16 = keep.tile([P, P], BF16, name="ident_bf16")
@@ -82,6 +84,7 @@ def tile_crosslayertranscoder_kernel(tc, x, W_enc, b_enc, b_dec, W_dec, dec_mask
         dec_raw = {}
         dec_grouped = {}
         dec_passed = {}
+        bdec_spread = []
         dec_codes = {}
         acc = {}
         staged = {}
@@ -116,10 +119,6 @@ def tile_crosslayertranscoder_kernel(tc, x, W_enc, b_enc, b_dec, W_dec, dec_mask
             if r < n_pairs:
                 load_dec(2 * r)
                 load_dec(2 * r + 1)
-            if r == BDEC_ROUND:
-                nc.sync.dma_start(
-                    out=bdec[:], in_=b_dec.rearrange("l d -> (l d)").partition_broadcast(P)
-                )
             if r + 1 < n_enc:
                 load_enc(r + 1)
 
@@ -227,19 +226,34 @@ def tile_crosslayertranscoder_kernel(tc, x, W_enc, b_enc, b_dec, W_dec, dec_mask
             )
             dec_passed[r] = passed
 
+        def spread_bdec():
+            for half in range(2):
+                spread = acc_pool.tile([P, 2, D], BF16, name="spread", tag="acc%d_0" % (half + 1))
+                for e in range(2):
+                    row = L * G + 2 * half + e
+                    nc.tensor.matmul(
+                        out=spread[:, e, :],
+                        lhsT=ident_bf16[:, row : row + 1].to_broadcast([P, P]),
+                        rhs=benc_rows[:],
+                        start=True,
+                        stop=True,
+                    )
+                bdec_spread.append(spread)
+
         def start_pair(r):
             grouped = grouped_pool.tile(
                 [P, 2, D, PACK], BF16, name="dec_grouped", tag="dec_grouped", align_bytes=64
             )
             dec_grouped[r] = grouped
-            nc.scalar.copy(out=grouped[:, 0, 0:PASSED_COLUMNS, :], in_=dec_passed[r][:])
+            if r < PASSED_PAIRS:
+                nc.scalar.copy(out=grouped[:, 0, 0:PASSED_COLUMNS, :], in_=dec_passed[r][:])
 
         def interleave_pair(r):
             grouped = dec_grouped[r]
             for h in range(2):
                 raw = dec_raw[2 * r + h]
                 split = SCALAR_COLUMNS[r][h]
-                done = PASSED_COLUMNS if h == 0 else 0
+                done = PASSED_COLUMNS if h == 0 and r < PASSED_PAIRS else 0
                 if split > done:
                     interleave_columns(nc.scalar.copy, grouped, h, raw, done, split)
                 if split < D:
@@ -315,19 +329,26 @@ def tile_crosslayertranscoder_kernel(tc, x, W_enc, b_enc, b_dec, W_dec, dec_mask
                 empty_transposes(r)
             if r < n_pairs:
                 start_pair(r)
+            if r in BDEC_ROUNDS:
+                half = BDEC_ROUNDS.index(r)
+                nc.scalar.copy(
+                    out=bdec[:, half * 2 * D : (half + 1) * 2 * D],
+                    in_=bdec_spread[half][:].rearrange("p e d -> p (e d)"),
+                )
             if 0 <= n < n_enc:
                 quantize_chunk(n)
             if 1 <= n < n_enc:
                 encode_chunk(n)
             if r + 1 < n_enc:
                 transpose_chunk(r + 1)
-            if r + 1 < n_pairs:
+            if r + 1 < PASSED_PAIRS:
                 pass_columns(r + 1)
             if r == 1:
                 for u in range(2):
                     nc.tensor.transpose(
                         benc_turned[:, u, :], every_2nd_word(benc_rows[:], u), ident[:]
                     )
+                spread_bdec()
             if finished is not None:
                 relu_layer(finished)
             if r < n_pairs:

@@ -49,7 +49,7 @@ def tile_crosslayertranscoder_kernel(tc, x, W_enc, b_enc, b_dec, W_dec, dec_mask
         raw_pool = ctx.enter_context(tc.tile_pool(name="raw_pool", bufs=3 * (LOOKAHEAD + 1)))
         enc_pool = ctx.enter_context(tc.tile_pool(name="enc_pool", bufs=2))
         act_pool = ctx.enter_context(tc.tile_pool(name="act_pool", bufs=2))
-        out_pool = ctx.enter_context(tc.tile_pool(name="out_pool", bufs=2))
+        out_pool = ctx.enter_context(tc.tile_pool(name="out_pool", bufs=L))
         grouped_pool = ctx.enter_context(tc.tile_pool(name="grouped_pool", bufs=3))
         code_pool = ctx.enter_context(tc.tile_pool(name="code_pool", bufs=5))
         turn_pool = ctx.enter_context(tc.psum_pool(name="turn_pool", bufs=2))
@@ -301,7 +301,10 @@ def tile_crosslayertranscoder_kernel(tc, x, W_enc, b_enc, b_dec, W_dec, dec_mask
                         closed.append((j, lo, hi))
             return closed
 
-        def add_bdec_and_store(j, lo, hi):
+        def store(j):
+            nc.sync.dma_start(out=out[j], in_=staged[j][:])
+
+        def add_bdec(j, lo, hi):
             if j not in staged:
                 staged[j] = out_pool.tile([P, D], F32, name="staged", tag="staged")
             nc.vector.tensor_tensor(
@@ -310,8 +313,6 @@ def tile_crosslayertranscoder_kernel(tc, x, W_enc, b_enc, b_dec, W_dec, dec_mask
                 in1=bdec[:, j * D + lo : j * D + hi],
                 op=ADD,
             )
-            if lo == 0:
-                nc.sync.dma_start(out=out[j], in_=staged[j][:])
 
         benc_turned = bank_pool.tile([P, 2, P], F32, name="benc_turned", tag="bank")
         for r in range(LOOKAHEAD):
@@ -321,8 +322,14 @@ def tile_crosslayertranscoder_kernel(tc, x, W_enc, b_enc, b_dec, W_dec, dec_mask
 
         next_pair = 0
         outputs_due = {}
+        stores_waiting = []
         for r in range(n_pairs + 1):
             load_for_round(r + LOOKAHEAD)
+            loads_are_queued = r + LOOKAHEAD >= n_pairs - 1
+            if loads_are_queued:
+                for j in stores_waiting:
+                    store(j)
+                stores_waiting.clear()
             n = r - 1
             finished = layer_finished_in.get(r)
             if r < n_enc:
@@ -380,4 +387,8 @@ def tile_crosslayertranscoder_kernel(tc, x, W_enc, b_enc, b_dec, W_dec, dec_mask
             if 1 <= n < n_enc:
                 add_benc(n)
             for j, lo, hi in outputs_due.get(r, []):
-                add_bdec_and_store(j, lo, hi)
+                add_bdec(j, lo, hi)
+                if lo == 0 and loads_are_queued:
+                    store(j)
+                elif lo == 0:
+                    stores_waiting.append(j)

@@ -23,14 +23,14 @@ FLOPS = 2 * L * T * F * D + 2 * N_BLOCKS * T * F * D
 BYTES = 2 * (L * T * D + L * F * D + L * F + L * D + N_BLOCKS * F * D) + 4 * L * T * D
 
 LOOKAHEAD = 4
-BDEC_ROUNDS = (2, 3)
+BDEC_ROUNDS = (3, 4)
 FIRST_OUTPUT_ROUND = 6
 MAX_PAIRS_A_ROUND = 2
 RUN = 4
 PASSED_COLUMNS = 128
-PASSED_PAIRS = 12
+PASSED_CHUNKS = [0] * 2 + [1] * 10 + [2] * 3
 SCALAR_COLUMNS = (
-    [(192, 0), (448, 0), (512, 0), (512, 0), (512, 64)]
+    [(192, 0), (448, 0), (512, 64), (512, 0), (512, 0)]
     + [(512, 208), (512, 160), (512, 64), (512, 208), (512, 160)]
     + [(512, 64), (512, 208), (512, 64), (512, 384), (512, 320)]
 )
@@ -216,28 +216,28 @@ def tile_crosslayertranscoder_kernel(tc, x, W_enc, b_enc, b_dec, W_dec, dec_mask
             )
 
         def pass_columns(r):
-            passed = passed_pool.tile([P, PASSED_COLUMNS, PACK], BF16, name="passed", tag="passed")
-            nc.tensor.matmul(
-                out=passed[:],
-                lhsT=ident_bf16[:],
-                rhs=dec_raw[2 * r][:, :, 0:PASSED_COLUMNS].rearrange("p t d -> p d t"),
-                start=True,
-                stop=True,
-            )
+            passed = passed_pool.tile([P, 2, PASSED_COLUMNS, PACK], BF16, name="passed", tag="passed")
+            for h in range(PASSED_CHUNKS[r]):
+                nc.tensor.matmul(
+                    out=passed[:, h, :, :],
+                    lhsT=ident_bf16[:],
+                    rhs=dec_raw[2 * r + h][:, :, 0:PASSED_COLUMNS].rearrange("p t d -> p d t"),
+                    start=True,
+                    stop=True,
+                )
             dec_passed[r] = passed
 
         def spread_bdec():
             for half in range(2):
                 spread = acc_pool.tile([P, 2, D], BF16, name="spread", tag="acc%d_0" % (half + 1))
                 for e in range(2):
-                    row = L * G + 2 * half + e
-                    nc.tensor.matmul(
-                        out=spread[:, e, :],
-                        lhsT=ident_bf16[:, row : row + 1].to_broadcast([P, P]),
-                        rhs=benc_rows[:],
-                        start=True,
-                        stop=True,
-                    )
+                    j = 2 * half + e
+                    for c in range(D // P):
+                        nc.tensor.transpose(
+                            spread[:, e, c * P : (c + 1) * P],
+                            bdec_cols[:, c, j : j + 1].to_broadcast([P, P]),
+                            ident_bf16[:],
+                        )
                 bdec_spread.append(spread)
 
         def start_pair(r):
@@ -245,15 +245,18 @@ def tile_crosslayertranscoder_kernel(tc, x, W_enc, b_enc, b_dec, W_dec, dec_mask
                 [P, 2, D, PACK], BF16, name="dec_grouped", tag="dec_grouped", align_bytes=64
             )
             dec_grouped[r] = grouped
-            if r < PASSED_PAIRS:
-                nc.scalar.copy(out=grouped[:, 0, 0:PASSED_COLUMNS, :], in_=dec_passed[r][:])
+            count = PASSED_CHUNKS[r]
+            if count > 0:
+                nc.scalar.copy(
+                    out=grouped[:, 0:count, 0:PASSED_COLUMNS, :], in_=dec_passed[r][:, 0:count, :, :]
+                )
 
         def interleave_pair(r):
             grouped = dec_grouped[r]
             for h in range(2):
                 raw = dec_raw[2 * r + h]
-                split = SCALAR_COLUMNS[r][h]
-                done = PASSED_COLUMNS if h == 0 and r < PASSED_PAIRS else 0
+                done = PASSED_COLUMNS if h < PASSED_CHUNKS[r] else 0
+                split = max(SCALAR_COLUMNS[r][h], done)
                 if split > done:
                     interleave_columns(nc.scalar.copy, grouped, h, raw, done, split)
                 if split < D:
@@ -315,10 +318,11 @@ def tile_crosslayertranscoder_kernel(tc, x, W_enc, b_enc, b_dec, W_dec, dec_mask
             )
 
         benc_turned = bank_pool.tile([P, 2, P], F32, name="benc_turned", tag="bank")
+        bdec_turned = acc_pool.tile([P, D // P, P], BF16, name="bdec_turned", tag="acc3_%d" % HALF)
+        bdec_cols = keep.tile([P, D // P, L], BF16, name="bdec_cols")
         for r in range(LOOKAHEAD):
             load_for_round(r)
         transpose_chunk(0)
-        pass_columns(0)
 
         next_pair = 0
         outputs_due = {}
@@ -344,18 +348,29 @@ def tile_crosslayertranscoder_kernel(tc, x, W_enc, b_enc, b_dec, W_dec, dec_mask
                 )
             if 0 <= n < n_enc:
                 quantize_chunk(n)
+            if r == 2:
+                nc.vector.tensor_copy(
+                    out=benc[:].bitcast(F32),
+                    in_=benc_turned[:, :, 0 : L * G].rearrange("p u c -> p c u"),
+                )
+                nc.vector.tensor_copy(out=bdec_cols[:], in_=bdec_turned[:, :, L * G : L * G + L])
             if 1 <= n < n_enc:
                 encode_chunk(n)
             if r + 1 < n_enc:
                 transpose_chunk(r + 1)
-            if r + 1 < PASSED_PAIRS:
+            if r + 1 < n_pairs and PASSED_CHUNKS[r + 1] > 0:
                 pass_columns(r + 1)
+            if r == 2:
+                spread_bdec()
             if r == 1:
                 for u in range(2):
                     nc.tensor.transpose(
                         benc_turned[:, u, :], every_2nd_word(benc_rows[:], u), ident[:]
                     )
-                spread_bdec()
+                for c in range(D // P):
+                    nc.tensor.transpose(
+                        bdec_turned[:, c, :], benc_rows[:, c * P : (c + 1) * P], ident_bf16[:]
+                    )
             if finished is not None:
                 relu_layer(finished)
             if r < n_pairs:
@@ -364,11 +379,6 @@ def tile_crosslayertranscoder_kernel(tc, x, W_enc, b_enc, b_dec, W_dec, dec_mask
                 quantize_pair(r - 1, ((0, 2 * D),))
             if r == n_pairs:
                 quantize_pair(r - 1, ((0, D),))
-            if r == 1:
-                nc.vector.tensor_copy(
-                    out=benc[:].bitcast(F32),
-                    in_=benc_turned[:, :, 0 : L * G].rearrange("p u c -> p c u"),
-                )
             if finished is not None:
                 quantize_acts(finished)
             if r == n_pairs:

@@ -23,6 +23,7 @@ FLOPS = 2 * L * T * F * D + 2 * N_BLOCKS * T * F * D
 BYTES = 2 * (L * T * D + L * F * D + L * F + L * D + N_BLOCKS * F * D) + 4 * L * T * D
 
 LOOKAHEAD = 4
+DMA_ALIGN = 256
 BDEC_ROUNDS = (3, 4)
 FIRST_OUTPUT_ROUND = 6
 MAX_PAIRS_A_ROUND = 2
@@ -91,10 +92,10 @@ def tile_crosslayertranscoder_kernel(tc, x, W_enc, b_enc, b_dec, W_dec, dec_mask
 
         def load_enc(n):
             if n == 0:
-                raw = keep.tile([P, L, D], BF16, name="x_raw")
+                raw = keep.tile([P, L, D], BF16, name="x_raw", align_bytes=DMA_ALIGN)
                 rows = x.rearrange("l t k -> t l k")
             else:
-                raw = raw_pool.tile([P, PACK, D], BF16, name="raw", tag="raw")
+                raw = raw_pool.tile([P, PACK, D], BF16, name="raw", tag="raw", align_bytes=DMA_ALIGN)
                 l, g = enc_chunks[n]
                 rows = W_enc[l, g * K_PASS : (g + 1) * K_PASS, :].rearrange(
                     "(m s) k -> m s k", s=PACK
@@ -104,7 +105,7 @@ def tile_crosslayertranscoder_kernel(tc, x, W_enc, b_enc, b_dec, W_dec, dec_mask
 
         def load_dec(c):
             i, j, g = dec_chunks[c]
-            raw = raw_pool.tile([P, PACK, D], BF16, name="raw", tag="raw")
+            raw = raw_pool.tile([P, PACK, D], BF16, name="raw", tag="raw", align_bytes=DMA_ALIGN)
             nc.sync.dma_start(
                 out=raw[:],
                 in_=W_dec[i, j, g * K_PASS : (g + 1) * K_PASS, :].rearrange(
@@ -304,12 +305,14 @@ def tile_crosslayertranscoder_kernel(tc, x, W_enc, b_enc, b_dec, W_dec, dec_mask
                         closed.append((j, lo, hi))
             return closed
 
-        def store(j):
-            nc.sync.dma_start(out=out[j], in_=staged[j][:])
+        def store(j, lo, hi):
+            nc.sync.dma_start(out=out[j][:, lo:hi], in_=staged[j][:, lo:hi])
 
         def add_bdec(j, lo, hi):
             if j not in staged:
-                staged[j] = out_pool.tile([P, D], F32, name="staged", tag="staged")
+                staged[j] = out_pool.tile(
+                    [P, D], F32, name="staged", tag="staged", align_bytes=DMA_ALIGN
+                )
             nc.vector.tensor_tensor(
                 out=staged[j][:, lo:hi],
                 in0=acc[(j, lo)][:],
@@ -331,8 +334,8 @@ def tile_crosslayertranscoder_kernel(tc, x, W_enc, b_enc, b_dec, W_dec, dec_mask
             load_for_round(r + LOOKAHEAD)
             loads_are_queued = r + LOOKAHEAD >= n_pairs - 1
             if loads_are_queued:
-                for j in stores_waiting:
-                    store(j)
+                for group in stores_waiting:
+                    store(*group)
                 stores_waiting.clear()
             n = r - 1
             finished = layer_finished_in.get(r)
@@ -398,7 +401,7 @@ def tile_crosslayertranscoder_kernel(tc, x, W_enc, b_enc, b_dec, W_dec, dec_mask
                 add_benc(n)
             for j, lo, hi in outputs_due.get(r, []):
                 add_bdec(j, lo, hi)
-                if lo == 0 and loads_are_queued:
-                    store(j)
-                elif lo == 0:
-                    stores_waiting.append(j)
+                if loads_are_queued:
+                    store(j, lo, hi)
+                else:
+                    stores_waiting.append((j, lo, hi))

@@ -100,7 +100,11 @@ def tile_crosslayertranscoder_kernel(tc, x, W_enc, b_enc, b_dec, W_dec, dec_mask
                 rows = W_enc[l, g * K_PASS : (g + 1) * K_PASS, :].rearrange(
                     "(m s) k -> m s k", s=PACK
                 )
-            nc.sync.dma_start(out=raw[:], in_=rows)
+            if n == 0:
+                for l in range(L):
+                    nc.sync.dma_start(out=raw[:, l, :], in_=rows[:, l, :])
+            else:
+                nc.sync.dma_start(out=raw[:], in_=rows)
             enc_raw[n] = raw
 
         def load_dec(c):

@@ -47,7 +47,7 @@ def tile_crosslayertranscoder_kernel(tc, x, W_enc, b_enc, b_dec, W_dec, dec_mask
 
     with ExitStack() as ctx:
         keep = ctx.enter_context(tc.tile_pool(name="keep", bufs=1))
-        raw_pool = ctx.enter_context(tc.tile_pool(name="raw_pool", bufs=3 * (LOOKAHEAD + 1)))
+        raw_pool = ctx.enter_context(tc.tile_pool(name="raw_pool", bufs=3 * (LOOKAHEAD + 2)))
         enc_pool = ctx.enter_context(tc.tile_pool(name="enc_pool", bufs=2))
         act_pool = ctx.enter_context(tc.tile_pool(name="act_pool", bufs=2))
         out_pool = ctx.enter_context(tc.tile_pool(name="out_pool", bufs=L))
@@ -310,7 +310,10 @@ def tile_crosslayertranscoder_kernel(tc, x, W_enc, b_enc, b_dec, W_dec, dec_mask
             return closed
 
         def store(j, lo, hi):
-            nc.sync.dma_start(out=out[j][:, lo:hi], in_=staged[j][:, lo:hi])
+            for first in range(lo, hi, HALF):
+                nc.sync.dma_start(
+                    out=out[j][:, first : first + HALF], in_=staged[j][:, first : first + HALF]
+                )
 
         def add_bdec(j, lo, hi):
             if j not in staged:

@@ -59,8 +59,12 @@ def tile_crosslayertranscoder_kernel(tc, x, W_enc, b_enc, b_dec, W_dec, dec_mask
         passed_pool = ctx.enter_context(tc.psum_pool(name="passed_pool", bufs=1))
         ctx.enter_context(tc.manual_schedule())
 
+        warm_in = keep.tile([P, 1], F32, name="warm_in")
+        warm_out = keep.tile([P, 1], F32, name="warm_out")
+        nc.vector.memset(warm_in[:], 0.0)
+        nc.scalar.copy(out=warm_out[:], in_=warm_in[:])
         benc_rows = keep.tile([P, K_PASS], BF16, name="benc_rows")
-        nc.gpsimd.memset(benc_rows[:], 0.0)
+        nc.vector.memset(benc_rows[:], 0.0)
         nc.scalar.dma_start(
             out=benc_rows[0 : L * G, :], in_=b_enc.rearrange("l (g c) -> (l g) c", g=G)
         )
@@ -119,10 +123,11 @@ def tile_crosslayertranscoder_kernel(tc, x, W_enc, b_enc, b_dec, W_dec, dec_mask
             dec_raw[c] = raw
 
         def load_for_round(r):
+            if r < n_pairs:
+                load_dec(2 * r)
             if r == 0:
                 load_enc(0)
             if r < n_pairs:
-                load_dec(2 * r)
                 load_dec(2 * r + 1)
             if r + 1 < n_enc:
                 load_enc(r + 1)
@@ -256,9 +261,9 @@ def tile_crosslayertranscoder_kernel(tc, x, W_enc, b_enc, b_dec, W_dec, dec_mask
                     out=grouped[:, 0:count, 0:PASSED_COLUMNS, :], in_=dec_passed[r][:, 0:count, :, :]
                 )
 
-        def interleave_pair(r):
+        def interleave_pair(r, chunks):
             grouped = dec_grouped[r]
-            for h in range(2):
+            for h in chunks:
                 raw = dec_raw[2 * r + h]
                 done = PASSED_COLUMNS if h < PASSED_CHUNKS[r] else 0
                 split = max(SCALAR_COLUMNS[r][h], done)
@@ -346,9 +351,12 @@ def tile_crosslayertranscoder_kernel(tc, x, W_enc, b_enc, b_dec, W_dec, dec_mask
                 stores_waiting.clear()
             n = r - 1
             finished = layer_finished_in.get(r)
+            if r == 0:
+                start_pair(r)
+                interleave_pair(r, (0,))
             if r < n_enc:
                 empty_transposes(r)
-            if r < n_pairs:
+            if 0 < r < n_pairs:
                 start_pair(r)
             if r in BDEC_ROUNDS:
                 half = BDEC_ROUNDS.index(r)
@@ -384,7 +392,7 @@ def tile_crosslayertranscoder_kernel(tc, x, W_enc, b_enc, b_dec, W_dec, dec_mask
             if finished is not None:
                 relu_layer(finished)
             if r < n_pairs:
-                interleave_pair(r)
+                interleave_pair(r, (1,) if r == 0 else (0, 1))
             if 1 <= r < n_pairs:
                 quantize_pair(r - 1, ((0, 2 * D),))
             if r == n_pairs:

@@ -74,6 +74,7 @@ def tile_crosslayertranscoder_kernel(tc, x, W_enc, b_enc, b_dec, W_dec, dec_mask
         ident_bf16 = keep.tile([P, P], BF16, name="ident_bf16")
         make_identity(nc, ident_bf16[:])
         benc = keep.tile([P, L * G, PACK], BF16, name="benc")
+        benc_twice = keep.tile([P, L * G, PACK, 2], BF16, name="benc_twice")
         bdec = keep.tile([P, L * D], BF16, name="bdec")
         x_codes = keep.tile([P, L * T], U32, name="x_codes", align_bytes=64)
         x_scales = keep.tile([P, L * T], U8, name="x_scales", align_bytes=64)
@@ -194,18 +195,20 @@ def tile_crosslayertranscoder_kernel(tc, x, W_enc, b_enc, b_dec, W_dec, dec_mask
         def add_benc(n):
             l, g = enc_chunks[n]
             if g == 0:
-                biased[l] = act_pool.tile([P, G, T, PACK], BF16, name="biased", tag="biased")
+                biased[l] = act_pool.tile([P, G, T // 2, PACK, 2], BF16, name="biased", tag="biased")
             nc.vector.tensor_tensor(
-                out=biased[l][:, g, :, :],
-                in0=enc_bank[n][:].rearrange("p s n -> p n s"),
-                in1=benc[:, n - 1 : n, :].to_broadcast([P, T, PACK]),
+                out=biased[l][:, g, :, :, :],
+                in0=enc_bank[n][:].rearrange("p s (a e) -> p a s e", e=2),
+                in1=benc_twice[:, n - 1 : n, :, :].to_broadcast([P, T // 2, PACK, 2]),
                 op=ADD,
             )
 
         def relu_layer(l):
             acts[l] = act_pool.tile([P, G * T * PACK], BF16, name="acts", tag="acts", align_bytes=64)
             nc.vector.tensor_scalar_max(
-                out=acts[l][:], in0=biased[l][:].rearrange("p g n s -> p (g n s)"), scalar1=0.0
+                out=acts[l][:].rearrange("p (x e s) -> p x e s", e=2, s=PACK),
+                in0=biased[l][:].rearrange("p g a s e -> p (g a) e s"),
+                scalar1=0.0,
             )
 
         def quantize_acts(l):
@@ -372,6 +375,10 @@ def tile_crosslayertranscoder_kernel(tc, x, W_enc, b_enc, b_dec, W_dec, dec_mask
                     in_=benc_turned[:, :, 0 : L * G].rearrange("p u c -> p c u"),
                 )
                 nc.vector.tensor_copy(out=bdec_cols[:], in_=bdec_turned[:, :, L * G : L * G + L])
+                nc.vector.tensor_copy(
+                    out=benc_twice[:].rearrange("p c s e -> p (c s) e"),
+                    in_=benc[:].rearrange("p c s -> p (c s)").unsqueeze(2).to_broadcast([P, L * G * PACK, 2]),
+                )
             if 1 <= n < n_enc:
                 encode_chunk(n)
             if r + 1 < n_enc:

@@ -32,8 +32,8 @@ PASSED_COLUMNS = 128
 PASSED_CHUNKS = [0] * 2 + [1] * 10 + [2] * 3
 SCALAR_COLUMNS = (
     [(192, 0), (448, 0), (512, 64), (512, 0), (512, 0)]
-    + [(512, 208), (512, 160), (512, 64), (512, 208), (512, 160)]
-    + [(512, 64), (512, 208), (512, 64), (512, 384), (512, 320)]
+    + [(512, 208), (512, 128), (512, 0), (512, 208), (512, 160)]
+    + [(512, 0), (512, 208), (512, 0), (512, 384), (512, 320)]
 )
 
 

@@ -31,7 +31,7 @@ RUN = 4
 PASSED_COLUMNS = 128
 PASSED_CHUNKS = [0] * 2 + [1] * 10 + [2] * 3
 SCALAR_COLUMNS = (
-    [(192, 0), (448, 0), (512, 64), (512, 0), (512, 0)]
+    [(192, 0), (384, 0), (512, 0), (448, 0), (448, 0)]
     + [(512, 208), (512, 128), (512, 0), (512, 208), (512, 160)]
     + [(512, 0), (512, 208), (512, 0), (512, 384), (512, 320)]
 )

from contextlib import ExitStack

import concourse.mybir as mybir
from concourse.masks import make_identity

F32 = mybir.dt.float32
BF16 = mybir.dt.bfloat16
U32 = mybir.dt.uint32
U8 = mybir.dt.uint8
FP8X4 = mybir.dt.float8_e4m3fn_x4
ADD = mybir.AluOpType.add

L, T, F, D = 4, 128, 1536, 512
P = 128
PACK = 4
K_PASS = P * PACK
G = F // K_PASS
HALF = D // 2
ENC_BANK = BF16

N_BLOCKS = L * (L + 1) // 2
FLOPS = 2 * L * T * F * D + 2 * N_BLOCKS * T * F * D
BYTES = 2 * (L * T * D + L * F * D + L * F + L * D + N_BLOCKS * F * D) + 4 * L * T * D

LOOKAHEAD = 4
DMA_ALIGN = 256
BDEC_ROUNDS = (3, 4)
FIRST_OUTPUT_ROUND = 6
MAX_PAIRS_A_ROUND = 2
RUN = 4
PASSED_COLUMNS = 128
PASSED_CHUNKS = [0] * 2 + [1] * 10 + [2] * 3
SCALAR_COLUMNS = (
    [(192, 0), (384, 0), (512, 0), (448, 0), (448, 0)]
    + [(512, 208), (512, 128), (512, 0), (512, 208), (512, 160)]
    + [(512, 0), (512, 208), (512, 0), (512, 384), (512, 320)]
)


def tile_crosslayertranscoder_kernel(tc, x, W_enc, b_enc, b_dec, W_dec, dec_mask, out):
    nc = tc.nc
    enc_chunks = [None] + [(l, g) for l in range(L) for g in range(G)]
    dec_chunks = [(i, j, g) for i in range(L) for j in range(i, L) for g in range(G)]
    n_enc = len(enc_chunks)
    n_pairs = len(dec_chunks) // 2
    layer_finished_in = {G * l + G + 2: l for l in range(L)}

    with ExitStack() as ctx:
        keep = ctx.enter_context(tc.tile_pool(name="keep", bufs=1))
        raw_pool = ctx.enter_context(tc.tile_pool(name="raw_pool", bufs=3 * (LOOKAHEAD + 2)))
        enc_pool = ctx.enter_context(tc.tile_pool(name="enc_pool", bufs=2))
        act_pool = ctx.enter_context(tc.tile_pool(name="act_pool", bufs=2))
        out_pool = ctx.enter_context(tc.tile_pool(name="out_pool", bufs=L))
        grouped_pool = ctx.enter_context(tc.tile_pool(name="grouped_pool", bufs=3))
        code_pool = ctx.enter_context(tc.tile_pool(name="code_pool", bufs=5))
        turn_pool = ctx.enter_context(tc.psum_pool(name="turn_pool", bufs=2))
        bank_pool = ctx.enter_context(tc.psum_pool(name="bank_pool", bufs=1))
        acc_pool = ctx.enter_context(tc.psum_pool(name="acc_pool", bufs=1))
        passed_pool = ctx.enter_context(tc.psum_pool(name="passed_pool", bufs=1))
        ctx.enter_context(tc.manual_schedule())

        warm_in = keep.tile([P, 1], F32, name="warm_in")
        warm_out = keep.tile([P, 1], F32, name="warm_out")
        nc.vector.memset(warm_in[:], 0.0)
        nc.scalar.copy(out=warm_out[:], in_=warm_in[:])
        benc_rows = keep.tile([P, K_PASS], BF16, name="benc_rows")
        nc.vector.memset(benc_rows[:], 0.0)
        nc.scalar.dma_start(
            out=benc_rows[0 : L * G, :], in_=b_enc.rearrange("l (g c) -> (l g) c", g=G)
        )
        nc.scalar.dma_start(out=benc_rows[L * G : L * G + L, :], in_=b_dec)
        ident = keep.tile([P, P], F32, name="ident")
        make_identity(nc, ident[:])
        ident_bf16 = keep.tile([P, P], BF16, name="ident_bf16")
        make_identity(nc, ident_bf16[:])
        benc = keep.tile([P, L * G, PACK], BF16, name="benc")
        benc_twice = keep.tile([P, L * G, PACK, 2], BF16, name="benc_twice")
        bdec = keep.tile([P, L * D], BF16, name="bdec")
        x_codes = keep.tile([P, L * T], U32, name="x_codes", align_bytes=64)
        x_scales = keep.tile([P, L * T], U8, name="x_scales", align_bytes=64)

        enc_raw = {}
        enc_turned = {}
        enc_grouped = {}
        enc_codes = {0: (x_codes, x_scales)}
        enc_bank = {}
        biased = {}
        acts = {}
        act_codes = {}
        dec_raw = {}
        dec_grouped = {}
        dec_passed = {}
        bdec_spread = []
        dec_codes = {}
        acc = {}
        staged = {}

        def load_enc(n):
            if n == 0:
                raw = keep.tile([P, L, D], BF16, name="x_raw", align_bytes=DMA_ALIGN)
                rows = x.rearrange("l t k -> t l k")
            else:
                raw = raw_pool.tile([P, PACK, D], BF16, name="raw", tag="raw", align_bytes=DMA_ALIGN)
                l, g = enc_chunks[n]
                rows = W_enc[l, g * K_PASS : (g + 1) * K_PASS, :].rearrange(
                    "(m s) k -> m s k", s=PACK
                )
            if n == 0:
                for l in range(L):
                    nc.sync.dma_start(out=raw[:, l, :], in_=rows[:, l, :])
            else:
                nc.sync.dma_start(out=raw[:], in_=rows)
            enc_raw[n] = raw

        def load_dec(c):
            i, j, g = dec_chunks[c]
            raw = raw_pool.tile([P, PACK, D], BF16, name="raw", tag="raw", align_bytes=DMA_ALIGN)
            nc.sync.dma_start(
                out=raw[:],
                in_=W_dec[i, j, g * K_PASS : (g + 1) * K_PASS, :].rearrange(
                    "(p t) d -> p t d", t=PACK
                ),
            )
            dec_raw[c] = raw

        def load_for_round(r):
            if r < n_pairs:
                load_dec(2 * r)
            if r == 0:
                load_enc(0)
            if r < n_pairs:
                load_dec(2 * r + 1)
            if r + 1 < n_enc:
                load_enc(r + 1)

        def every_2nd_word(row_of_k, u):
            return row_of_k.bitcast(F32)[:, u : D // 2 : 2]

        def transpose_chunk(n):
            banks = []
            for h in range(2):
                turned = turn_pool.tile([P, 2, 2, P], F32, name="turned", tag="turned")
                for s in range(2):
                    for u in range(2):
                        nc.tensor.transpose(
                            turned[:, s, u, :],
                            every_2nd_word(enc_raw[n][:, 2 * h + s, :], u),
                            ident[:],
                        )
                banks.append(turned)
            enc_turned[n] = banks

        def empty_transposes(n):
            grouped = enc_pool.tile(
                [P, PACK, P, PACK], BF16, name="enc_grouped", tag="enc_grouped", align_bytes=64
            )
            words = grouped[:].bitcast(F32)
            for h in range(2):
                nc.scalar.copy(
                    out=words[:, 2 * h : 2 * h + 2, :, :],
                    in_=enc_turned[n][h][:].rearrange("q s u m -> q s m u"),
                )
            enc_grouped[n] = grouped

        def quantize_chunk(n):
            if n > 0:
                codes = enc_pool.tile([P, K_PASS], U32, name="w_codes", tag="w_codes", align_bytes=64)
                scales = enc_pool.tile(
                    [P, K_PASS], U8, name="w_scales", tag="w_scales", align_bytes=64
                )
                enc_codes[n] = (codes, scales)
            codes, scales = enc_codes[n]
            nc.vector.quantize_mx(
                out=codes[:].bitcast(FP8X4),
                scales=scales[:],
                in_=enc_grouped[n][:].rearrange("q s m j -> q (s m j)"),
            )

        def encode_chunk(n):
            l, g = enc_chunks[n]
            codes, scales = enc_codes[n]
            bank = bank_pool.tile([P, PACK, T], ENC_BANK, name="bank", tag="bank")
            for s in range(PACK):
                nc.tensor.matmul_mx(
                    out=bank[:, s, :],
                    lhsT=codes[:, s * P : (s + 1) * P].bitcast(FP8X4),
                    lhsT_scale=scales[:, s * P : (s + 1) * P],
                    rhs=x_codes[:, l * T : (l + 1) * T].bitcast(FP8X4),
                    rhs_scale=x_scales[:, l * T : (l + 1) * T],
                    start=True,
                    stop=True,
                )
            enc_bank[n] = bank

        def add_benc(n):
            l, g = enc_chunks[n]
            if g == 0:
                biased[l] = act_pool.tile([P, G, T // 2, PACK, 2], BF16, name="biased", tag="biased")
            nc.vector.tensor_tensor(
                out=biased[l][:, g, :, :, :],
                in0=enc_bank[n][:].rearrange("p s (a e) -> p a s e", e=2),
                in1=benc_twice[:, n - 1 : n, :, :].to_broadcast([P, T // 2, PACK, 2]),
                op=ADD,
            )

        def relu_layer(l):
            acts[l] = act_pool.tile([P, G * T * PACK], BF16, name="acts", tag="acts", align_bytes=64)
            nc.vector.tensor_scalar_max(
                out=acts[l][:].rearrange("p (x e s) -> p x e s", e=2, s=PACK),
                in0=biased[l][:].rearrange("p g a s e -> p (g a) e s"),
                scalar1=0.0,
            )

        def quantize_acts(l):
            codes = keep.tile([P, G * T], U32, name="a_codes%d" % l, align_bytes=64)
            scales = keep.tile([P, G * T], U8, name="a_scales%d" % l, align_bytes=64)
            for lo, hi in ((0, 2 * T), (2 * T, 3 * T)):
                nc.vector.quantize_mx(
                    out=codes[:, lo:hi].bitcast(FP8X4),
                    scales=scales[:, lo:hi],
                    in_=acts[l][:, lo * PACK : hi * PACK],
                )
            act_codes[l] = (codes, scales)

        def interleave_columns(engine_copy, grouped, h, raw, lo, hi):
            engine_copy(
                out=grouped[:, h, lo:hi, :].rearrange("p (c i) t -> p c t i", i=RUN),
                in_=raw[:, :, lo:hi].rearrange("p t (c i) -> p c t i", i=RUN),
            )

        def pass_columns(r):
            passed = passed_pool.tile([P, 2, PASSED_COLUMNS, PACK], BF16, name="passed", tag="passed")
            for h in range(PASSED_CHUNKS[r]):
                nc.tensor.matmul(
                    out=passed[:, h, :, :],
                    lhsT=ident_bf16[:],
                    rhs=dec_raw[2 * r + h][:, :, 0:PASSED_COLUMNS].rearrange("p t d -> p d t"),
                    start=True,
                    stop=True,
                )
            dec_passed[r] = passed

        def spread_bdec():
            for half in range(2):
                spread = acc_pool.tile([P, 2, D], BF16, name="spread", tag="acc%d_0" % (half + 1))
                for e in range(2):
                    j = 2 * half + e
                    for c in range(D // P):
                        nc.tensor.transpose(
                            spread[:, e, c * P : (c + 1) * P],
                            bdec_cols[:, c, j : j + 1].to_broadcast([P, P]),
                            ident_bf16[:],
                        )
                bdec_spread.append(spread)

        def start_pair(r):
            grouped = grouped_pool.tile(
                [P, 2, D, PACK], BF16, name="dec_grouped", tag="dec_grouped", align_bytes=64
            )
            dec_grouped[r] = grouped
            count = PASSED_CHUNKS[r]
            if count > 0:
                nc.scalar.copy(
                    out=grouped[:, 0:count, 0:PASSED_COLUMNS, :], in_=dec_passed[r][:, 0:count, :, :]
                )

        def interleave_pair(r, chunks):
            grouped = dec_grouped[r]
            for h in chunks:
                raw = dec_raw[2 * r + h]
                done = PASSED_COLUMNS if h < PASSED_CHUNKS[r] else 0
                split = max(SCALAR_COLUMNS[r][h], done)
                if split > done:
                    interleave_columns(nc.scalar.copy, grouped, h, raw, done, split)
                if split < D:
                    interleave_columns(nc.vector.tensor_copy, grouped, h, raw, split, D)

        def quantize_pair(r, pieces):
            if r not in dec_codes:
                codes = code_pool.tile([P, 2 * D], U32, name="d_codes", tag="d_codes", align_bytes=64)
                scales = code_pool.tile(
                    [P, 2 * D], U8, name="d_scales", tag="d_scales", align_bytes=64
                )
                dec_codes[r] = (codes, scales)
            codes, scales = dec_codes[r]
            grouped = dec_grouped[r][:].rearrange("p h d t -> p (h d t)")
            for lo, hi in pieces:
                nc.vector.quantize_mx(
                    out=codes[:, lo:hi].bitcast(FP8X4),
                    scales=scales[:, lo:hi],
                    in_=grouped[:, lo * PACK : hi * PACK],
                )

        def decode_pair(r):
            closed = []
            codes, scales = dec_codes[r]
            for h in range(2):
                i, j, g = dec_chunks[2 * r + h]
                first = i == 0 and g == 0
                final = i == j and g == G - 1
                parts = ((0, D),) if j < L - 1 else ((HALF, D), (0, HALF))
                a_codes, a_scales = act_codes[i]
                for lo, hi in parts:
                    if first:
                        bank_of = "acc0_0" if (j, lo) == (L - 1, 0) else "acc%d_%d" % (j, lo)
                        acc[(j, lo)] = acc_pool.tile([P, hi - lo], F32, name="acc", tag=bank_of)
                    nc.tensor.matmul_mx(
                        out=acc[(j, lo)][:],
                        lhsT=a_codes[:, g * T : (g + 1) * T].bitcast(FP8X4),
                        lhsT_scale=a_scales[:, g * T : (g + 1) * T],
                        rhs=codes[:, h * D + lo : h * D + hi].bitcast(FP8X4),
                        rhs_scale=scales[:, h * D + lo : h * D + hi],
                        start=first,
                        stop=final,
                    )
                    if final:
                        closed.append((j, lo, hi))
            return closed

        def store(j, lo, hi):
            for first in range(lo, hi, HALF):
                nc.sync.dma_start(
                    out=out[j][:, first : first + HALF], in_=staged[j][:, first : first + HALF]
                )

        def add_bdec(j, lo, hi):
            if j not in staged:
                staged[j] = out_pool.tile(
                    [P, D], F32, name="staged", tag="staged", align_bytes=DMA_ALIGN
                )
            nc.vector.tensor_tensor(
                out=staged[j][:, lo:hi],
                in0=acc[(j, lo)][:],
                in1=bdec[:, j * D + lo : j * D + hi],
                op=ADD,
            )

        benc_turned = bank_pool.tile([P, 2, P], F32, name="benc_turned", tag="bank")
        bdec_turned = acc_pool.tile([P, D // P, P], BF16, name="bdec_turned", tag="acc3_%d" % HALF)
        bdec_cols = keep.tile([P, D // P, L], BF16, name="bdec_cols")
        for r in range(LOOKAHEAD):
            load_for_round(r)
        transpose_chunk(0)

        next_pair = 0
        outputs_due = {}
        stores_waiting = []
        for r in range(n_pairs + 1):
            load_for_round(r + LOOKAHEAD)
            loads_are_queued = r + LOOKAHEAD >= n_pairs - 1
            if loads_are_queued:
                for group in stores_waiting:
                    store(*group)
                stores_waiting.clear()
            n = r - 1
            finished = layer_finished_in.get(r)
            if r == 0:
                start_pair(r)
                interleave_pair(r, (0,))
            if r < n_enc:
                empty_transposes(r)
            if 0 < r < n_pairs:
                start_pair(r)
            if r in BDEC_ROUNDS:
                half = BDEC_ROUNDS.index(r)
                nc.scalar.copy(
                    out=bdec[:, half * 2 * D : (half + 1) * 2 * D],
                    in_=bdec_spread[half][:].rearrange("p e d -> p (e d)"),
                )
            if 0 <= n < n_enc:
                quantize_chunk(n)
            if r == 2:
                nc.vector.tensor_copy(
                    out=benc[:].bitcast(F32),
                    in_=benc_turned[:, :, 0 : L * G].rearrange("p u c -> p c u"),
                )
                nc.vector.tensor_copy(out=bdec_cols[:], in_=bdec_turned[:, :, L * G : L * G + L])
                nc.vector.tensor_copy(
                    out=benc_twice[:].rearrange("p c s e -> p (c s) e"),
                    in_=benc[:].rearrange("p c s -> p (c s)").unsqueeze(2).to_broadcast([P, L * G * PACK, 2]),
                )
            if 1 <= n < n_enc:
                encode_chunk(n)
            if r + 1 < n_enc:
                transpose_chunk(r + 1)
            if r + 1 < n_pairs and PASSED_CHUNKS[r + 1] > 0:
                pass_columns(r + 1)
            if r == 2:
                spread_bdec()
            if r == 1:
                for u in range(2):
                    nc.tensor.transpose(
                        benc_turned[:, u, :], every_2nd_word(benc_rows[:], u), ident[:]
                    )
                for c in range(D // P):
                    nc.tensor.transpose(
                        bdec_turned[:, c, :], benc_rows[:, c * P : (c + 1) * P], ident_bf16[:]
                    )
            if finished is not None:
                relu_layer(finished)
            if r < n_pairs:
                interleave_pair(r, (1,) if r == 0 else (0, 1))
            if 1 <= r < n_pairs:
                quantize_pair(r - 1, ((0, 2 * D),))
            if r == n_pairs:
                quantize_pair(r - 1, ((0, D),))
            if finished is not None:
                quantize_acts(finished)
            if r == n_pairs:
                quantize_pair(r - 1, ((D + HALF, 2 * D), (D, D + HALF)))
            written = 0
            while (
                written < MAX_PAIRS_A_ROUND
                and next_pair < r
                and all(dec_chunks[2 * next_pair + h][0] in act_codes for h in range(2))
            ):
                for group in decode_pair(next_pair):
                    when = r if r == n_pairs else max(r + 1, FIRST_OUTPUT_ROUND)
                    outputs_due.setdefault(when, []).append(group)
                next_pair += 1
                written += 1
            if 1 <= n < n_enc:
                add_benc(n)
            for j, lo, hi in outputs_due.get(r, []):
                add_bdec(j, lo, hi)
                if loads_are_queued:
                    store(j, lo, hi)
                else:
                    stores_waiting.append((j, lo, hi))
